import numpy as np
import ml_dtypes


def mxq(x, axis, fmt="e4m3"):
    dtype, down = {"e4m3": (ml_dtypes.float8_e4m3fn, 7), "e5m2": (ml_dtypes.float8_e5m2, 14)}[fmt]
    v = np.moveaxis(np.asarray(x, np.float32).astype(ml_dtypes.bfloat16).astype(np.float64), axis, -1)
    blocks = v.reshape(v.shape[:-1] + (-1, 32))
    amax = np.abs(blocks).max(-1, keepdims=True)
    byte = np.maximum(np.where(amax > 0, np.frexp(amax)[1] - 1 + 127, 0) - down, 1)
    scale = np.exp2(byte - 127.0)
    codes = (blocks / scale).astype(np.float32).astype(dtype).astype(np.float64)
    return np.moveaxis((codes * scale).reshape(v.shape), -1, axis)


WIDE = False


def mx_kscale(k):
    if not WIDE:
        return np.ones(k)
    levels = np.array([10, -10, 5, -5, 0])
    if k % 512:
        return np.exp2(np.random.permutation(np.resize(levels, k // 32))).repeat(32)
    a = np.empty((k // 512, 16))
    for p in range(k // 512):
        a[p, :8] = np.random.permutation(np.resize(levels, 8))
        for g in range(8):
            far = levels[np.abs(levels - a[p, g]) >= 10]
            a[p, g + 8] = far[np.random.randint(len(far))]
    return np.exp2(a.ravel()).repeat(32)


BF16 = ml_dtypes.bfloat16


def bf(x):
    return np.asarray(x, np.float32).astype(BF16)


def f64(x):
    return np.asarray(x).astype(np.float64)


B, C, H, W = 1, 1024, 32, 32
INTER = C // 2
HW = H * W
HW2 = HW // 2
SP = np.sqrt(2.0 / np.sqrt(C))


def draw0():
    s = mx_kscale(C)
    t = mx_kscale(INTER)
    return {"q": bf(np.random.standard_normal((B, C, H, W)) * s[None, :, None, None]),
            "k": bf(np.random.standard_normal((B, C, H, W)) * s[None, :, None, None]),
            "W_phi": bf(np.random.standard_normal((INTER, C)) * SP / np.sqrt(C) * t[:, None] / s[None, :]),
            "W_theta": bf(np.random.standard_normal((INTER, C)) * SP / np.sqrt(C) / t[:, None] / s[None, :])}


def core(q, k, W_phi, W_theta):
    qf = f64(q).reshape(B, C, HW)
    kf = f64(k).reshape(B, C, HW)
    phi = (mxq(f64(W_phi), 1, "e4m3") @ mxq(qf, 1, "e4m3")).reshape(B, C, HW2)
    theta = (mxq(f64(W_theta), 1, "e4m3") @ mxq(kf, 1, "e4m3")).reshape(B, C, HW2)
    return mxq(theta, 1, "e4m3").transpose(0, 2, 1) @ mxq(phi, 1, "e4m3")


def e4m3fn_bytes(y):
    return np.clip(np.asarray(y, np.float64), -448.0, 448.0).astype(np.float32).astype(ml_dtypes.float8_e4m3fn).view(np.uint8)


def e4m3fn_values(b):
    return np.asarray(b, np.uint8).view(ml_dtypes.float8_e4m3fn).astype(np.float64)


def setup_inputs():
    d = draw0()
    x0 = np.asarray(d['q']).astype(np.float64)
    s = (np.max(np.abs(x0), axis=(0, 2, 3), keepdims=True) / 448.0).astype(np.float32)
    out = {}
    for k, v in d.items():
        if k == 'q':
            out['q_bytes'] = e4m3fn_bytes(x0 / s.astype(np.float64))
            out['q_scale'] = s
        else:
            out[k] = v
    return out


def reference(q_bytes, q_scale, k, W_phi, W_theta):
    return core(e4m3fn_values(q_bytes) * q_scale.astype(np.float64), k, W_phi, W_theta)

@@ -1,0 +1,268 @@
+from contextlib import ExitStack
+
+import concourse.mybir as mybir
+from concourse.masks import make_identity
+
+C, INTER, HW = 1024, 512, 1024
+FLOPS = 2 * (2 * INTER * C * HW) + 2 * (HW // 2) * (HW // 2) * C
+
+F32 = mybir.dt.float32
+BF16 = mybir.dt.bfloat16
+U32 = mybir.dt.uint32
+U8 = mybir.dt.uint8
+FP8 = mybir.dt.float8_e4m3fn
+FP8X4 = mybir.dt.float8_e4m3fn_x4
+COPY = mybir.ActivationFunctionType.Copy
+MULT = mybir.AluOpType.mult
+
+P = 128
+
+
+def tile_nonlocalblock_pa_kernel(tc, q_bytes, q_scale, k, W_phi, W_theta, out):
+    nc = tc.nc
+    q_rows = q_bytes.rearrange("a (h p t) y x -> h p (a t) (y x)", h=2, p=P, t=4)
+    s_rows = q_scale.rearrange("a (h p t) y x -> p h (a t y x)", h=2, p=P, t=4)
+    k_rows = k.rearrange("a (h p t) y x -> h p (a t) (y x)", h=2, p=P, t=4)
+    w_rows = {
+        "phi": W_phi.rearrange("(g m e) k -> g m e k", g=2, m=P, e=2),
+        "theta": W_theta.rearrange("(g m e) k -> g m e k", g=2, m=P, e=2),
+    }
+    out_rows = out.rearrange("a n m -> (a n) m")
+
+    with ExitStack() as ctx:
+        sb = ctx.enter_context(tc.tile_pool(name="sb", bufs=1))
+        psum = ctx.enter_context(tc.psum_pool(name="psum", bufs=8))
+        ctx.enter_context(tc.manual_schedule())
+
+        def tile(name, shape, dtype):
+            return sb.tile(shape, dtype, name=name, align_bytes=64)
+
+        scale = tile("scale", [P, 8], F32)
+        nc.scalar.dma_start(out=scale[:].rearrange("p (h t) -> p h t", h=2), in_=s_rows)
+        q8 = [tile("q8_%d" % h, [P, 4, HW], U8) for h in range(2)]
+        for h, t0, t1 in ((0, 0, 1), (0, 1, 2), (0, 2, 4), (1, 0, 4)):
+            nc.sync.dma_start(out=q8[h][:, t0:t1, :], in_=q_rows[h][:, t0:t1, :])
+        w_raw = {}
+        for w in ("phi", "theta"):
+            for g in range(2):
+                w_raw[w, g] = tile("w_raw_%s%d" % (w, g), [P, 2, C], BF16)
+                nc.sync.dma_start(out=w_raw[w, g][:], in_=w_rows[w][g])
+        k_raw = [tile("k_raw_%d" % h, [P, 4, HW], BF16) for h in range(2)]
+        for h in range(2):
+            nc.sync.dma_start(out=k_raw[h][:], in_=k_rows[h])
+
+        ident = tile("ident", [P, P], F32)
+        make_identity(nc, ident[:])
+        dummy = tile("dummy", [P, 1], F32)
+        nc.vector.memset(dummy[:], 0.0)
+        dummy2 = tile("dummy2", [P, 1], F32)
+        nc.scalar.activation(out=dummy2[:], in_=dummy[:], func=COPY)
+
+        wide = [tile("wide_%d" % h, [P, 4, HW], BF16) for h in range(2)]
+
+        def widen(eng, h, t):
+            src = q8[h][:, t, :].bitcast(FP8)
+            sc = scale[:, 4 * h + t : 4 * h + t + 1]
+            if eng == "S":
+                nc.scalar.activation(out=wide[h][:, t, :], in_=src, func=COPY, scale=sc)
+            else:
+                nc.vector.tensor_scalar(out=wide[h][:, t, :], in0=src, scalar1=sc, scalar2=None, op0=MULT)
+
+        def copy(eng, dst, src):
+            if eng == "S":
+                nc.scalar.copy(out=dst, in_=src)
+            else:
+                nc.vector.tensor_copy(out=dst, in_=src)
+
+        def quantize(codes, scales, grouped):
+            nc.vector.quantize_mx(out=codes.bitcast(FP8X4), scales=scales, in_=grouped)
+
+        grouped = {}
+        codes = {}
+        scales = {}
+
+        def interleave(eng, x, src, h, b, nb):
+            width = P * nb
+            if (x, b) not in grouped:
+                grouped[x, b] = tile("%s_il_%d" % (x, b), [P, 2, 2, width, 4], BF16)
+            dst = grouped[x, b][:, h].rearrange("p j (m i) t -> p j m t i", i=4)
+            s = src[h][:].rearrange("p t (j m i) -> p j m t i", j=2, i=4)[:, :, b * P // 4 : (b + nb) * P // 4]
+            copy(eng, dst, s)
+
+        def quantize_px(x, h0, h1, b, nb):
+            width = P * nb
+            if (x, b) not in codes:
+                codes[x, b] = tile("%s_c_%d" % (x, b), [P, 2, 2, width], U32)
+                scales[x, b] = tile("%s_s_%d" % (x, b), [P, 2, 2, width], U8)
+            quantize(
+                codes[x, b][:, h0:h1].rearrange("p h j n -> p (h j n)"),
+                scales[x, b][:, h0:h1].rearrange("p h j n -> p (h j n)"),
+                grouped[x, b][:, h0:h1].rearrange("p h j n t -> p (h j n t)"),
+            )
+
+        w_t = {}
+        w_c = {}
+        w_s = {}
+        w_bank = {}
+
+        def transpose_w(w, g, h):
+            words = w_raw[w, g][:].rearrange("p e k -> p (e k)").bitcast(F32)
+            bank = psum.tile([P, 2, 2, P], F32, name="bank")
+            for e in range(2):
+                for u in range(2):
+                    first = 512 * e + 256 * h + u
+                    nc.tensor.transpose(bank[:, e, u, :], words[:, first : first - u + 256 : 2], ident[:])
+            w_bank[w, g, h] = bank
+
+        def copy_w(eng, w, g, h):
+            if (w, g) not in w_t:
+                w_t[w, g] = tile("w_t_%s%d" % (w, g), [P, 2, 2, P, 2], F32)
+            copy(eng, w_t[w, g][:, h], w_bank[w, g, h][:].rearrange("p e u m -> p e m u"))
+
+        def quantize_w(w, g):
+            w_c[w, g] = tile("w_c_%s%d" % (w, g), [P, 2, 2, P], U32)
+            w_s[w, g] = tile("w_s_%s%d" % (w, g), [P, 2, 2, P], U8)
+            quantize(
+                w_c[w, g][:].rearrange("p h e m -> p (h e m)"),
+                w_s[w, g][:].rearrange("p h e m -> p (h e m)"),
+                w_t[w, g][:].rearrange("p h e m u -> p (h e m u)").bitcast(BF16),
+            )
+
+        p_bank = {}
+        fold = {}
+
+        def project(w, x, g, b, nb):
+            bank = psum.tile([P, 4, P], F32, name="bank")
+            n0 = P * (b % nb)
+            for e in range(2):
+                for j in range(2):
+                    for h in range(2):
+                        nc.tensor.matmul_mx(
+                            out=bank[:, 2 * e + j, :],
+                            lhsT=w_c[w, g][:, h, e, :].bitcast(FP8X4),
+                            lhsT_scale=w_s[w, g][:, h, e, :],
+                            rhs=codes[x, b - b % nb][:, h, j, n0 : n0 + P].bitcast(FP8X4),
+                            rhs_scale=scales[x, b - b % nb][:, h, j, n0 : n0 + P],
+                            start=(h == 0),
+                            stop=(h == 1),
+                        )
+            p_bank[w, g, b] = bank
+
+        phi_f = [tile("phi_f_%d" % g, [P, HW // 2, 4], BF16) for g in range(2)]
+        phi_c = [tile("phi_c_%d" % g, [P, HW // 2], U32) for g in range(2)]
+        phi_s = [tile("phi_s_%d" % g, [P, HW // 2], U8) for g in range(2)]
+        th_f = [tile("th_f_%d" % b, [P, 2, P, 4], BF16) for b in range(4)]
+        th_c = [tile("th_c_%d" % b, [P, 2, P], U32) for b in range(4)]
+        th_s = [tile("th_s_%d" % b, [P, 2, P], U8) for b in range(4)]
+
+        def copy_phi(eng, g, b):
+            copy(eng, phi_f[g][:, P * b : P * (b + 1), :], p_bank["phi", g, b][:].rearrange("p t n -> p n t"))
+
+        def quantize_phi(g):
+            quantize(phi_c[g][:], phi_s[g][:], phi_f[g][:].rearrange("p n t -> p (n t)"))
+
+        def copy_theta(eng, g, b):
+            copy(eng, th_f[b][:, g], p_bank["theta", g, b][:].rearrange("p t n -> p n t"))
+
+        def quantize_theta(b):
+            quantize(
+                th_c[b][:].rearrange("p g n -> p (g n)"),
+                th_s[b][:].rearrange("p g n -> p (g n)"),
+                th_f[b][:].rearrange("p g n t -> p (g n t)"),
+            )
+
+        def affinity(b, parts):
+            width = 512 // parts
+            for i in range(parts):
+                cols = slice(i * width, (i + 1) * width)
+                bank = psum.tile([P, width], F32, name="bank")
+                for g in range(2):
+                    nc.tensor.matmul_mx(
+                        out=bank[:],
+                        lhsT=th_c[b][:, g, :].bitcast(FP8X4),
+                        lhsT_scale=th_s[b][:, g, :],
+                        rhs=phi_c[g][:, cols].bitcast(FP8X4),
+                        rhs_scale=phi_s[g][:, cols],
+                        start=(g == 0),
+                        stop=(g == 1),
+                    )
+                p_bank["out", b, i] = bank
+
+        def store(engs, b):
+            parts = len(engs)
+            width = 512 // parts
+            for i, eng in enumerate(engs):
+                res = tile("res_%d%d" % (b, i), [P, width], F32)
+                copy(eng, res[:], p_bank["out", b, i][:])
+                (nc.scalar if i else nc.sync).dma_start(
+                    out=out_rows[P * b : P * (b + 1), i * width : (i + 1) * width], in_=res[:]
+                )
+
+        widen("S", 0, 0)
+        for t in (1, 2, 3):
+            widen("V", 0, t)
+        for t in (0, 1, 2):
+            widen("S", 1, t)
+        interleave("V", "q", wide, 0, 0, 2)
+        interleave("V", "q", wide, 0, 2, 2)
+        widen("V", 1, 3)
+        quantize_px("q", 0, 1, 0, 2)
+        quantize_px("q", 0, 1, 2, 2)
+        for w in ("phi", "theta"):
+            for g in range(2):
+                for h in range(2):
+                    transpose_w(w, g, h)
+        for g in range(2):
+            for h in range(2):
+                copy_w("S", "phi", g, h)
+        interleave("V", "q", wide, 1, 0, 2)
+        quantize_w("phi", 0)
+        quantize_px("q", 1, 2, 0, 2)
+        quantize_w("phi", 1)
+        interleave("V", "q", wide, 1, 2, 2)
+        for g in range(2):
+            for h in range(2):
+                copy_w("S", "theta", g, h)
+        interleave("V", "k", k_raw, 0, 0, 1)
+        quantize_px("q", 1, 2, 2, 2)
+        for b in range(4):
+            for g in range(2):
+                project("phi", "q", g, b, 2)
+                copy_phi("S", g, b)
+        interleave("V", "k", k_raw, 1, 0, 1)
+        quantize_w("theta", 0)
+        quantize_w("theta", 1)
+        quantize_px("k", 0, 2, 0, 1)
+
+        def theta(b, engs):
+            for g in range(2):
+                project("theta", "k", g, b, 1)
+                copy_theta(engs[g], g, b)
+
+        interleave("V", "k", k_raw, 0, 1, 1)
+        interleave("V", "k", k_raw, 1, 1, 1)
+        quantize_phi(0)
+        quantize_px("k", 0, 2, 1, 1)
+        theta(0, "SS")
+        interleave("V", "k", k_raw, 0, 2, 1)
+        quantize_theta(0)
+        interleave("V", "k", k_raw, 1, 2, 1)
+        quantize_phi(1)
+        quantize_px("k", 0, 2, 2, 1)
+        theta(1, "SS")
+        affinity(0, 1)
+        interleave("V", "k", k_raw, 0, 3, 1)
+        interleave("V", "k", k_raw, 1, 3, 1)
+        quantize_theta(1)
+        quantize_px("k", 0, 2, 3, 1)
+        store("S", 0)
+        theta(2, "SS")
+        quantize_theta(2)
+        affinity(1, 1)
+        store("S", 1)
+        theta(3, "SV")
+        quantize_theta(3)
+        affinity(2, 1)
+        store("S", 2)
+        affinity(3, 2)
+        store("SV", 3)

@@ -40,7 +40,7 @@ def tile_nonlocalblock_pa_kernel(tc, q_bytes, q_scale, k, W_phi, W_theta, out):
         scale = tile("scale", [P, 8], F32)
         nc.scalar.dma_start(out=scale[:].rearrange("p (h t) -> p h t", h=2), in_=s_rows)
         q8 = [tile("q8_%d" % h, [P, 4, HW], U8) for h in range(2)]
-        for h, t0, t1 in ((0, 0, 1), (0, 1, 2), (0, 2, 4), (1, 0, 4)):
+        for h, t0, t1 in ((0, 0, 1), (0, 1, 2), (0, 2, 4), (1, 0, 2), (1, 2, 4)):
             nc.sync.dma_start(out=q8[h][:, t0:t1, :], in_=q_rows[h][:, t0:t1, :])
         w_raw = {}
         for w in ("phi", "theta"):
@@ -203,66 +203,64 @@ def tile_nonlocalblock_pa_kernel(tc, q_bytes, q_scale, k, W_phi, W_theta, out):
             widen("V", 0, t)
         for t in (0, 1, 2):
             widen("S", 1, t)
-        interleave("V", "q", wide, 0, 0, 2)
-        interleave("V", "q", wide, 0, 2, 2)
-        widen("V", 1, 3)
-        quantize_px("q", 0, 1, 0, 2)
-        quantize_px("q", 0, 1, 2, 2)
         for w in ("phi", "theta"):
             for g in range(2):
                 for h in range(2):
                     transpose_w(w, g, h)
-        for g in range(2):
-            for h in range(2):
-                copy_w("S", "phi", g, h)
+                    copy_w("S", w, g, h)
+        interleave("V", "q", wide, 0, 0, 2)
+        widen("V", 1, 3)
+        interleave("V", "q", wide, 0, 2, 2)
+        quantize_px("q", 0, 1, 0, 2)
         interleave("V", "q", wide, 1, 0, 2)
-        quantize_w("phi", 0)
+        quantize_px("q", 0, 1, 2, 2)
         quantize_px("q", 1, 2, 0, 2)
-        quantize_w("phi", 1)
+        quantize_w("phi", 0)
         interleave("V", "q", wide, 1, 2, 2)
-        for g in range(2):
-            for h in range(2):
-                copy_w("S", "theta", g, h)
-        interleave("V", "k", k_raw, 0, 0, 1)
+        quantize_w("phi", 1)
         quantize_px("q", 1, 2, 2, 2)
-        for b in range(4):
+        quantize_w("theta", 0)
+
+        def phi(b, engs):
             for g in range(2):
                 project("phi", "q", g, b, 2)
-                copy_phi("S", g, b)
-        interleave("V", "k", k_raw, 1, 0, 1)
-        quantize_w("theta", 0)
-        quantize_w("theta", 1)
-        quantize_px("k", 0, 2, 0, 1)
+                copy_phi(engs[g], g, b)
 
         def theta(b, engs):
             for g in range(2):
                 project("theta", "k", g, b, 1)
                 copy_theta(engs[g], g, b)
 
-        interleave("V", "k", k_raw, 0, 1, 1)
+        interleave("V", "k", k_raw, 1, 0, 1)
+        quantize_w("theta", 1)
+        interleave("S", "k", k_raw, 0, 0, 1)
+        phi(0, "SS")
         interleave("V", "k", k_raw, 1, 1, 1)
-        quantize_phi(0)
-        quantize_px("k", 0, 2, 1, 1)
-        theta(0, "SS")
-        interleave("V", "k", k_raw, 0, 2, 1)
-        quantize_theta(0)
+        quantize_px("k", 0, 2, 0, 1)
+        interleave("S", "k", k_raw, 0, 1, 1)
+        phi(1, "SS")
         interleave("V", "k", k_raw, 1, 2, 1)
-        quantize_phi(1)
-        quantize_px("k", 0, 2, 2, 1)
-        theta(1, "SS")
-        affinity(0, 1)
+        quantize_px("k", 0, 2, 1, 1)
+        interleave("S", "k", k_raw, 0, 2, 1)
+        phi(2, "SS")
         interleave("V", "k", k_raw, 0, 3, 1)
+        phi(3, "SV")
+        quantize_px("k", 0, 2, 2, 1)
+        theta(0, "SS")
+        theta(1, "SS")
         interleave("V", "k", k_raw, 1, 3, 1)
-        quantize_theta(1)
+        quantize_phi(0)
         quantize_px("k", 0, 2, 3, 1)
-        store("S", 0)
         theta(2, "SS")
+        quantize_phi(1)
+        quantize_theta(0)
+        quantize_theta(1)
         quantize_theta(2)
-        affinity(1, 1)
-        store("S", 1)
-        theta(3, "SV")
-        quantize_theta(3)
-        affinity(2, 1)
-        store("S", 2)
+        theta(3, "SS")
+        for b in range(3):
+            affinity(b, 1)
+            if b == 0:
+                quantize_theta(3)
+            store("SSV"[b], b)
         affinity(3, 2)
         store("SV", 3)

@@ -21,7 +21,7 @@ P = 128
 def tile_nonlocalblock_pa_kernel(tc, q_bytes, q_scale, k, W_phi, W_theta, out):
     nc = tc.nc
     q_rows = q_bytes.rearrange("a (h p t) y x -> h p (a t) (y x)", h=2, p=P, t=4)
-    s_rows = q_scale.rearrange("a (h p t) y x -> p h (a t y x)", h=2, p=P, t=4)
+    s_rows = q_scale.rearrange("a (h p t) y x -> h p (a t y x)", h=2, p=P, t=4)
     k_rows = k.rearrange("a (h p t) y x -> h p (a t) (y x)", h=2, p=P, t=4)
     w_rows = {
         "phi": W_phi.rearrange("(g m e) k -> g m e k", g=2, m=P, e=2),
@@ -37,8 +37,9 @@ def tile_nonlocalblock_pa_kernel(tc, q_bytes, q_scale, k, W_phi, W_theta, out):
         def tile(name, shape, dtype):
             return sb.tile(shape, dtype, name=name, align_bytes=64)
 
-        scale = tile("scale", [P, 8], F32)
-        nc.scalar.dma_start(out=scale[:].rearrange("p (h t) -> p h t", h=2), in_=s_rows)
+        scale = [tile("scale_%d" % h, [P, 4], F32) for h in range(2)]
+        for h in range(2):
+            nc.scalar.dma_start(out=scale[h][:], in_=s_rows[h])
         q8 = [tile("q8_%d" % h, [P, 4, HW], U8) for h in range(2)]
         for h, t0, t1 in ((0, 0, 1), (0, 1, 2), (0, 2, 4), (1, 0, 2), (1, 2, 4)):
             nc.sync.dma_start(out=q8[h][:, t0:t1, :], in_=q_rows[h][:, t0:t1, :])
@@ -62,7 +63,7 @@ def tile_nonlocalblock_pa_kernel(tc, q_bytes, q_scale, k, W_phi, W_theta, out):
 
         def widen(eng, h, t):
             src = q8[h][:, t, :].bitcast(FP8)
-            sc = scale[:, 4 * h + t : 4 * h + t + 1]
+            sc = scale[h][:, t : t + 1]
             if eng == "S":
                 nc.scalar.activation(out=wide[h][:, t, :], in_=src, func=COPY, scale=sc)
             else:
@@ -129,7 +130,11 @@ def tile_nonlocalblock_pa_kernel(tc, q_bytes, q_scale, k, W_phi, W_theta, out):
             )
 
         p_bank = {}
-        fold = {}
+
+        def warm_up(n):
+            bank = psum.tile([P, 512], F32, name="bank")
+            for i in range(n):
+                nc.tensor.matmul(bank[:], lhsT=w_raw["phi", 0][:, 0, :P], rhs=w_raw["phi", 0][:, 0, :512], start=True, stop=True)
 
         def project(w, x, g, b, nb):
             bank = psum.tile([P, 4, P], F32, name="bank")
@@ -198,26 +203,29 @@ def tile_nonlocalblock_pa_kernel(tc, q_bytes, q_scale, k, W_phi, W_theta, out):
                     out=out_rows[P * b : P * (b + 1), i * width : (i + 1) * width], in_=res[:]
                 )
 
-        widen("S", 0, 0)
-        for t in (1, 2, 3):
-            widen("V", 0, t)
-        for t in (0, 1, 2):
-            widen("S", 1, t)
-        for w in ("phi", "theta"):
-            for g in range(2):
-                for h in range(2):
-                    transpose_w(w, g, h)
-                    copy_w("S", w, g, h)
-        interleave("V", "q", wide, 0, 0, 2)
-        widen("V", 1, 3)
+        for eng, h, t in (("S", 0, 0), ("V", 0, 1), ("S", 0, 2), ("V", 0, 3), ("V", 1, 1), ("V", 1, 0), ("S", 1, 2), ("V", 1, 3)):
+            widen(eng, h, t)
+        interleave("S", "q", wide, 0, 0, 2)
         interleave("V", "q", wide, 0, 2, 2)
-        quantize_px("q", 0, 1, 0, 2)
-        interleave("V", "q", wide, 1, 0, 2)
-        quantize_px("q", 0, 1, 2, 2)
-        quantize_px("q", 1, 2, 0, 2)
-        quantize_w("phi", 0)
         interleave("V", "q", wide, 1, 2, 2)
+        interleave("V", "q", wide, 1, 0, 2)
+        for g in range(2):
+            for h in range(2):
+                transpose_w("phi", g, h)
+                copy_w("S", "phi", g, h)
+        for g in range(2):
+            for h in range(2):
+                transpose_w("theta", g, h)
+        quantize_px("q", 0, 1, 2, 2)
+        quantize_px("q", 0, 1, 0, 2)
+        quantize_w("phi", 0)
+        quantize_px("q", 1, 2, 0, 2)
         quantize_w("phi", 1)
+        warm_up(3)
+        for g in range(2):
+            for h in range(2):
+                copy_w("S", "theta", g, h)
+            interleave("S", "k", k_raw, g, 2, 1)
         quantize_px("q", 1, 2, 2, 2)
         quantize_w("theta", 0)
 
@@ -231,36 +239,33 @@ def tile_nonlocalblock_pa_kernel(tc, q_bytes, q_scale, k, W_phi, W_theta, out):
                 project("theta", "k", g, b, 1)
                 copy_theta(engs[g], g, b)
 
-        interleave("V", "k", k_raw, 1, 0, 1)
-        quantize_w("theta", 1)
-        interleave("S", "k", k_raw, 0, 0, 1)
         phi(0, "SS")
+        phi(1, "SS")
+        phi(2, "SS")
+        interleave("V", "k", k_raw, 0, 0, 1)
+        interleave("V", "k", k_raw, 0, 1, 1)
+        interleave("V", "k", k_raw, 1, 0, 1)
         interleave("V", "k", k_raw, 1, 1, 1)
         quantize_px("k", 0, 2, 0, 1)
-        interleave("S", "k", k_raw, 0, 1, 1)
-        phi(1, "SS")
-        interleave("V", "k", k_raw, 1, 2, 1)
+        quantize_w("theta", 1)
         quantize_px("k", 0, 2, 1, 1)
-        interleave("S", "k", k_raw, 0, 2, 1)
-        phi(2, "SS")
-        interleave("V", "k", k_raw, 0, 3, 1)
-        phi(3, "SV")
-        quantize_px("k", 0, 2, 2, 1)
+        phi(3, "SS")
         theta(0, "SS")
-        theta(1, "SS")
+        interleave("V", "k", k_raw, 0, 3, 1)
+        quantize_px("k", 0, 2, 2, 1)
         interleave("V", "k", k_raw, 1, 3, 1)
         quantize_phi(0)
         quantize_px("k", 0, 2, 3, 1)
-        theta(2, "SS")
         quantize_phi(1)
+        theta(1, "SS")
+        theta(2, "SV")
         quantize_theta(0)
         quantize_theta(1)
+        theta(3, "SV")
         quantize_theta(2)
-        theta(3, "SS")
+        quantize_theta(3)
         for b in range(3):
             affinity(b, 1)
-            if b == 0:
-                quantize_theta(3)
             store("SSV"[b], b)
         affinity(3, 2)
         store("SV", 3)

from contextlib import ExitStack

import concourse.mybir as mybir
from concourse.masks import make_identity

C, INTER, HW = 1024, 512, 1024
FLOPS = 2 * (2 * INTER * C * HW) + 2 * (HW // 2) * (HW // 2) * C

F32 = mybir.dt.float32
BF16 = mybir.dt.bfloat16
U32 = mybir.dt.uint32
U8 = mybir.dt.uint8
FP8 = mybir.dt.float8_e4m3fn
FP8X4 = mybir.dt.float8_e4m3fn_x4
COPY = mybir.ActivationFunctionType.Copy
MULT = mybir.AluOpType.mult

P = 128


def tile_nonlocalblock_pa_kernel(tc, q_bytes, q_scale, k, W_phi, W_theta, out):
    nc = tc.nc
    q_rows = q_bytes.rearrange("a (h p t) y x -> h p (a t) (y x)", h=2, p=P, t=4)
    s_rows = q_scale.rearrange("a (h p t) y x -> h p (a t y x)", h=2, p=P, t=4)
    k_rows = k.rearrange("a (h p t) y x -> h p (a t) (y x)", h=2, p=P, t=4)
    w_rows = {
        "phi": W_phi.rearrange("(g m e) k -> g m e k", g=2, m=P, e=2),
        "theta": W_theta.rearrange("(g m e) k -> g m e k", g=2, m=P, e=2),
    }
    out_rows = out.rearrange("a n m -> (a n) m")

    with ExitStack() as ctx:
        sb = ctx.enter_context(tc.tile_pool(name="sb", bufs=1))
        psum = ctx.enter_context(tc.psum_pool(name="psum", bufs=8))
        ctx.enter_context(tc.manual_schedule())

        def tile(name, shape, dtype):
            return sb.tile(shape, dtype, name=name, align_bytes=64)

        scale = [tile("scale_%d" % h, [P, 4], F32) for h in range(2)]
        for h in range(2):
            nc.scalar.dma_start(out=scale[h][:], in_=s_rows[h])
        q8 = [tile("q8_%d" % h, [P, 4, HW], U8) for h in range(2)]
        for h, t0, t1 in ((0, 0, 1), (0, 1, 2), (0, 2, 4), (1, 0, 2), (1, 2, 4)):
            nc.sync.dma_start(out=q8[h][:, t0:t1, :], in_=q_rows[h][:, t0:t1, :])
        w_raw = {}
        for w in ("phi", "theta"):
            for g in range(2):
                w_raw[w, g] = tile("w_raw_%s%d" % (w, g), [P, 2, C], BF16)
                nc.sync.dma_start(out=w_raw[w, g][:], in_=w_rows[w][g])
        k_raw = [tile("k_raw_%d" % h, [P, 4, HW], BF16) for h in range(2)]
        for h in range(2):
            nc.sync.dma_start(out=k_raw[h][:], in_=k_rows[h])

        ident = tile("ident", [P, P], F32)
        make_identity(nc, ident[:])
        dummy = tile("dummy", [P, 1], F32)
        nc.vector.memset(dummy[:], 0.0)
        dummy2 = tile("dummy2", [P, 1], F32)
        nc.scalar.activation(out=dummy2[:], in_=dummy[:], func=COPY)

        wide = [tile("wide_%d" % h, [P, 4, HW], BF16) for h in range(2)]

        def widen(eng, h, t):
            src = q8[h][:, t, :].bitcast(FP8)
            sc = scale[h][:, t : t + 1]
            if eng == "S":
                nc.scalar.activation(out=wide[h][:, t, :], in_=src, func=COPY, scale=sc)
            else:
                nc.vector.tensor_scalar(out=wide[h][:, t, :], in0=src, scalar1=sc, scalar2=None, op0=MULT)

        def copy(eng, dst, src):
            if eng == "S":
                nc.scalar.copy(out=dst, in_=src)
            else:
                nc.vector.tensor_copy(out=dst, in_=src)

        def quantize(codes, scales, grouped):
            nc.vector.quantize_mx(out=codes.bitcast(FP8X4), scales=scales, in_=grouped)

        grouped = {}
        codes = {}
        scales = {}

        def interleave(eng, x, src, h, b, nb):
            width = P * nb
            if (x, b) not in grouped:
                grouped[x, b] = tile("%s_il_%d" % (x, b), [P, 2, 2, width, 4], BF16)
            dst = grouped[x, b][:, h].rearrange("p j (m i) t -> p j m t i", i=4)
            s = src[h][:].rearrange("p t (j m i) -> p j m t i", j=2, i=4)[:, :, b * P // 4 : (b + nb) * P // 4]
            copy(eng, dst, s)

        def quantize_px(x, h0, h1, b, nb):
            width = P * nb
            if (x, b) not in codes:
                codes[x, b] = tile("%s_c_%d" % (x, b), [P, 2, 2, width], U32)
                scales[x, b] = tile("%s_s_%d" % (x, b), [P, 2, 2, width], U8)
            quantize(
                codes[x, b][:, h0:h1].rearrange("p h j n -> p (h j n)"),
                scales[x, b][:, h0:h1].rearrange("p h j n -> p (h j n)"),
                grouped[x, b][:, h0:h1].rearrange("p h j n t -> p (h j n t)"),
            )

        w_t = {}
        w_c = {}
        w_s = {}
        w_bank = {}

        def transpose_w(w, g, h):
            words = w_raw[w, g][:].rearrange("p e k -> p (e k)").bitcast(F32)
            bank = psum.tile([P, 2, 2, P], F32, name="bank")
            for e in range(2):
                for u in range(2):
                    first = 512 * e + 256 * h + u
                    nc.tensor.transpose(bank[:, e, u, :], words[:, first : first - u + 256 : 2], ident[:])
            w_bank[w, g, h] = bank

        def copy_w(eng, w, g, h):
            if (w, g) not in w_t:
                w_t[w, g] = tile("w_t_%s%d" % (w, g), [P, 2, 2, P, 2], F32)
            copy(eng, w_t[w, g][:, h], w_bank[w, g, h][:].rearrange("p e u m -> p e m u"))

        def quantize_w(w, g):
            w_c[w, g] = tile("w_c_%s%d" % (w, g), [P, 2, 2, P], U32)
            w_s[w, g] = tile("w_s_%s%d" % (w, g), [P, 2, 2, P], U8)
            quantize(
                w_c[w, g][:].rearrange("p h e m -> p (h e m)"),
                w_s[w, g][:].rearrange("p h e m -> p (h e m)"),
                w_t[w, g][:].rearrange("p h e m u -> p (h e m u)").bitcast(BF16),
            )

        p_bank = {}

        def warm_up(n):
            bank = psum.tile([P, 512], F32, name="bank")
            for i in range(n):
                nc.tensor.matmul(bank[:], lhsT=w_raw["phi", 0][:, 0, :P], rhs=w_raw["phi", 0][:, 0, :512], start=True, stop=True)

        def project(w, x, g, b, nb):
            bank = psum.tile([P, 4, P], F32, name="bank")
            n0 = P * (b % nb)
            for e in range(2):
                for j in range(2):
                    for h in range(2):
                        nc.tensor.matmul_mx(
                            out=bank[:, 2 * e + j, :],
                            lhsT=w_c[w, g][:, h, e, :].bitcast(FP8X4),
                            lhsT_scale=w_s[w, g][:, h, e, :],
                            rhs=codes[x, b - b % nb][:, h, j, n0 : n0 + P].bitcast(FP8X4),
                            rhs_scale=scales[x, b - b % nb][:, h, j, n0 : n0 + P],
                            start=(h == 0),
                            stop=(h == 1),
                        )
            p_bank[w, g, b] = bank

        phi_f = [tile("phi_f_%d" % g, [P, HW // 2, 4], BF16) for g in range(2)]
        phi_c = [tile("phi_c_%d" % g, [P, HW // 2], U32) for g in range(2)]
        phi_s = [tile("phi_s_%d" % g, [P, HW // 2], U8) for g in range(2)]
        th_f = [tile("th_f_%d" % b, [P, 2, P, 4], BF16) for b in range(4)]
        th_c = [tile("th_c_%d" % b, [P, 2, P], U32) for b in range(4)]
        th_s = [tile("th_s_%d" % b, [P, 2, P], U8) for b in range(4)]

        def copy_phi(eng, g, b):
            copy(eng, phi_f[g][:, P * b : P * (b + 1), :], p_bank["phi", g, b][:].rearrange("p t n -> p n t"))

        def quantize_phi(g):
            quantize(phi_c[g][:], phi_s[g][:], phi_f[g][:].rearrange("p n t -> p (n t)"))

        def copy_theta(eng, g, b):
            copy(eng, th_f[b][:, g], p_bank["theta", g, b][:].rearrange("p t n -> p n t"))

        def quantize_theta(b):
            quantize(
                th_c[b][:].rearrange("p g n -> p (g n)"),
                th_s[b][:].rearrange("p g n -> p (g n)"),
                th_f[b][:].rearrange("p g n t -> p (g n t)"),
            )

        def affinity(b, parts):
            width = 512 // parts
            for i in range(parts):
                cols = slice(i * width, (i + 1) * width)
                bank = psum.tile([P, width], F32, name="bank")
                for g in range(2):
                    nc.tensor.matmul_mx(
                        out=bank[:],
                        lhsT=th_c[b][:, g, :].bitcast(FP8X4),
                        lhsT_scale=th_s[b][:, g, :],
                        rhs=phi_c[g][:, cols].bitcast(FP8X4),
                        rhs_scale=phi_s[g][:, cols],
                        start=(g == 0),
                        stop=(g == 1),
                    )
                p_bank["out", b, i] = bank

        def store(engs, b):
            parts = len(engs)
            width = 512 // parts
            for i, eng in enumerate(engs):
                res = tile("res_%d%d" % (b, i), [P, width], F32)
                copy(eng, res[:], p_bank["out", b, i][:])
                (nc.scalar if i else nc.sync).dma_start(
                    out=out_rows[P * b : P * (b + 1), i * width : (i + 1) * width], in_=res[:]
                )

        for eng, h, t in (("S", 0, 0), ("V", 0, 1), ("S", 0, 2), ("V", 0, 3), ("V", 1, 1), ("V", 1, 0), ("S", 1, 2), ("V", 1, 3)):
            widen(eng, h, t)
        interleave("S", "q", wide, 0, 0, 2)
        interleave("V", "q", wide, 0, 2, 2)
        interleave("V", "q", wide, 1, 2, 2)
        interleave("V", "q", wide, 1, 0, 2)
        for g in range(2):
            for h in range(2):
                transpose_w("phi", g, h)
                copy_w("S", "phi", g, h)
        for g in range(2):
            for h in range(2):
                transpose_w("theta", g, h)
        quantize_px("q", 0, 1, 2, 2)
        quantize_px("q", 0, 1, 0, 2)
        quantize_w("phi", 0)
        quantize_px("q", 1, 2, 0, 2)
        quantize_w("phi", 1)
        warm_up(3)
        for g in range(2):
            for h in range(2):
                copy_w("S", "theta", g, h)
            interleave("S", "k", k_raw, g, 2, 1)
        quantize_px("q", 1, 2, 2, 2)
        quantize_w("theta", 0)

        def phi(b, engs):
            for g in range(2):
                project("phi", "q", g, b, 2)
                copy_phi(engs[g], g, b)

        def theta(b, engs):
            for g in range(2):
                project("theta", "k", g, b, 1)
                copy_theta(engs[g], g, b)

        phi(0, "SS")
        phi(1, "SS")
        phi(2, "SS")
        interleave("V", "k", k_raw, 0, 0, 1)
        interleave("V", "k", k_raw, 0, 1, 1)
        interleave("V", "k", k_raw, 1, 0, 1)
        interleave("V", "k", k_raw, 1, 1, 1)
        quantize_px("k", 0, 2, 0, 1)
        quantize_w("theta", 1)
        quantize_px("k", 0, 2, 1, 1)
        phi(3, "SS")
        theta(0, "SS")
        interleave("V", "k", k_raw, 0, 3, 1)
        quantize_px("k", 0, 2, 2, 1)
        interleave("V", "k", k_raw, 1, 3, 1)
        quantize_phi(0)
        quantize_px("k", 0, 2, 3, 1)
        quantize_phi(1)
        theta(1, "SS")
        theta(2, "SV")
        quantize_theta(0)
        quantize_theta(1)
        theta(3, "SV")
        quantize_theta(2)
        quantize_theta(3)
        for b in range(3):
            affinity(b, 1)
            store("SSV"[b], b)
        affinity(3, 2)
        store("SV", 3)
